import numpy as np
import ml_dtypes


def mxq(x, axis, fmt="e4m3"):
    dtype, down = {"e4m3": (ml_dtypes.float8_e4m3fn, 7), "e5m2": (ml_dtypes.float8_e5m2, 14)}[fmt]
    v = np.moveaxis(np.asarray(x, np.float32).astype(ml_dtypes.bfloat16).astype(np.float64), axis, -1)
    blocks = v.reshape(v.shape[:-1] + (-1, 32))
    amax = np.abs(blocks).max(-1, keepdims=True)
    byte = np.maximum(np.where(amax > 0, np.frexp(amax)[1] - 1 + 127, 0) - down, 1)
    scale = np.exp2(byte - 127.0)
    codes = (blocks / scale).astype(np.float32).astype(dtype).astype(np.float64)
    return np.moveaxis((codes * scale).reshape(v.shape), -1, axis)


WIDE = False


def mx_kscale(k):
    if not WIDE:
        return np.ones(k)
    levels = np.array([10, -10, 5, -5, 0])
    a = np.random.permutation(np.resize(levels, k // 512 * 4)).reshape(k // 512, 4)
    idx = np.arange(k)
    return np.exp2(a[idx // 512, idx % 128 // 32])


BF16 = ml_dtypes.bfloat16


def bf(x):
    return np.asarray(x, np.float32).astype(BF16)


def f64(x):
    return np.asarray(x).astype(np.float64)


E2M1 = np.array([0.0, 0.5, 1.0, 1.5, 2.0, 3.0, 4.0, 6.0, -0.0, -0.5, -1.0, -1.5, -2.0, -3.0, -4.0, -6.0])


def pack_weight(w, fmt):
    k, n = w.shape
    w = f64(bf(w)).reshape(k // 32, 32, n)
    amax = np.abs(w).max(1)
    if fmt == "e4m3":
        byte = np.frexp(amax)[1] - 1 + 127 - 7
    else:
        mant, ex = np.frexp(amax / 6.0)
        byte = np.where(mant > 0.5, ex, ex - 1) + 127
    byte = np.clip(np.where(amax > 0, byte, 1), 1, 254)
    scaled = (w * np.exp2(127.0 - byte)[:, None, :]).reshape(k, n).astype(np.float32)
    by_word = np.ascontiguousarray(scaled.reshape(k // 512, 128, 4, n).transpose(0, 1, 3, 2))
    if fmt == "e4m3":
        words = by_word.astype(ml_dtypes.float8_e4m3fn).view(np.uint8)
    else:
        c = by_word.astype(ml_dtypes.float4_e2m1fn).view(np.uint8) & 0xF
        words = c[..., 0::2] | (c[..., 1::2] << 4)
    return np.ascontiguousarray(words), np.ascontiguousarray(byte.astype(np.uint8).reshape(k // 512, 16, n))


def unpack_weight(words, scales, fmt):
    g, p, n, _ = words.shape
    if fmt == "e4m3":
        vals = np.ascontiguousarray(words).view(ml_dtypes.float8_e4m3fn).astype(np.float64)
    else:
        nib = np.empty((g, p, n, 4), np.uint8)
        nib[..., 0::2] = words & 0xF
        nib[..., 1::2] = words >> 4
        vals = E2M1[nib]
    vals = vals * np.repeat(np.exp2(scales.astype(np.float64) - 127.0), 8, axis=1)[..., None]
    return vals.transpose(0, 1, 3, 2).reshape(g * 512, n)


B, I, H = 128, 7936, 256
K = H + I
FMT = "e4m3"
NAMES = ["w_f_light", "w_i_light", "w_c_light", "w_o_light",
         "w_f_light_temp", "w_i_light_temp", "w_c_light_temp", "w_o_light_temp"]


def sigmoid(v):
    return 1.0 / (1.0 + np.exp(-v))


def setup_inputs():
    s = mx_kscale(K)
    inp = {
        "y": bf(np.random.standard_normal((B, I)) * s[H:]),
        "h_light": bf(np.random.standard_normal((B, H)) * s[:H]),
        "c_light": bf(np.random.standard_normal((B, H))),
        "h_temp": bf(np.random.standard_normal((B, H)) * s[:H]),
        "c_temp": bf(np.random.standard_normal((B, H))),
    }
    for n in NAMES:
        w = np.random.standard_normal((H, K)) / np.sqrt(K) / s
        words, scales = pack_weight(np.ascontiguousarray(w.T), FMT)
        inp[n + "_words"] = words
        inp[n + "_scales"] = scales
        inp["b" + n[1:]] = bf(np.random.standard_normal(H) * 0.5)
    return inp


def _branch(hx, wf, b_f, wi, b_i, wc, b_c, wo, b_o):
    W = np.concatenate([wf, wi, wc, wo], axis=1)
    b = np.concatenate([b_f, b_i, b_c, b_o], axis=0)
    z = (mxq(hx, 1, "e4m3") @ W) + b
    zf, zi, zc, zo = np.split(z, 4, axis=1)
    return sigmoid(zf), sigmoid(zi), np.tanh(zc), sigmoid(zo)


def reference(y, h_light, c_light, h_temp, c_temp,
              w_f_light_words, w_f_light_scales, b_f_light, w_i_light_words, w_i_light_scales, b_i_light,
              w_c_light_words, w_c_light_scales, b_c_light, w_o_light_words, w_o_light_scales, b_o_light,
              w_f_light_temp_words, w_f_light_temp_scales, b_f_light_temp,
              w_i_light_temp_words, w_i_light_temp_scales, b_i_light_temp,
              w_c_light_temp_words, w_c_light_temp_scales, b_c_light_temp,
              w_o_light_temp_words, w_o_light_temp_scales, b_o_light_temp):
    y, h_light, c_light, h_temp = f64(y), f64(h_light), f64(c_light), f64(h_temp)
    hx_l = np.concatenate([h_light, y], axis=1)
    hx_t = np.concatenate([h_temp, y], axis=1)
    f1, i1, ch1, o1 = _branch(hx_l, unpack_weight(w_f_light_words, w_f_light_scales, FMT), f64(b_f_light),
                              unpack_weight(w_i_light_words, w_i_light_scales, FMT), f64(b_i_light),
                              unpack_weight(w_c_light_words, w_c_light_scales, FMT), f64(b_c_light),
                              unpack_weight(w_o_light_words, w_o_light_scales, FMT), f64(b_o_light))
    f2, i2, ch2, o2 = _branch(hx_t, unpack_weight(w_f_light_temp_words, w_f_light_temp_scales, FMT), f64(b_f_light_temp),
                              unpack_weight(w_i_light_temp_words, w_i_light_temp_scales, FMT), f64(b_i_light_temp),
                              unpack_weight(w_c_light_temp_words, w_c_light_temp_scales, FMT), f64(b_c_light_temp),
                              unpack_weight(w_o_light_temp_words, w_o_light_temp_scales, FMT), f64(b_o_light_temp))
    c_new = (f1 * c_light + i1 * ch1) + (f2 * c_light + i2 * ch2)
    h_new = (o1 + o2) * np.tanh(c_new)
    return h_new, c_new

@@ -1,0 +1,171 @@
+from contextlib import ExitStack
+
+import concourse.mybir as mybir
+from concourse.masks import make_identity
+
+F32 = mybir.dt.float32
+BF16 = mybir.dt.bfloat16
+I32 = mybir.dt.int32
+U32 = mybir.dt.uint32
+U8 = mybir.dt.uint8
+FP8X4 = mybir.dt.float8_e4m3fn_x4
+ACT = mybir.ActivationFunctionType
+
+P = 128
+H = 256
+K = 8192
+K_PASS = 512
+GROUPS = K // K_PASS
+WORDS = K_PASS // 2
+
+LIGHT, TEMP = 0, 1
+GATE_F, GATE_I, GATE_C, GATE_O = 0, 1, 2, 3
+
+GROUPS_PER_ROUND = 2
+GROUPS_PER_Y_LOAD = 4
+GROUPS_PER_W_LOAD = 4
+TEMP_SLOT = GROUPS
+
+FLOPS = 2 * P * K * 8 * H
+
+
+def tile_customlstmcell_k_kernel(tc, y, h_light, c_light, h_temp, c_temp, *weights_and_outs):
+    nc = tc.nc
+    w_words = [[weights_and_outs[3 * (4 * branch + gate)] for branch in (LIGHT, TEMP)] for gate in range(4)]
+    w_scales = [[weights_and_outs[3 * (4 * branch + gate) + 1] for branch in (LIGHT, TEMP)] for gate in range(4)]
+    w_bias = [[weights_and_outs[3 * (4 * branch + gate) + 2] for branch in (LIGHT, TEMP)] for gate in range(4)]
+    out_h, out_c = weights_and_outs[24], weights_and_outs[25]
+
+    with ExitStack() as ctx:
+        keep = ctx.enter_context(tc.tile_pool(name="keep", bufs=1))
+        stage = ctx.enter_context(tc.tile_pool(name="stage", bufs=3))
+        t_psum = ctx.enter_context(tc.psum_pool(name="t_psum", bufs=3))
+        b_psum = ctx.enter_context(tc.psum_pool(name="b_psum", bufs=2))
+        z_psum = ctx.enter_context(tc.psum_pool(name="z_psum", bufs=3))
+        ctx.enter_context(tc.manual_schedule())
+
+        hx_light = keep.tile([P, K], BF16)
+        hx_temp0 = keep.tile([P, K_PASS], BF16)
+        c_bf16 = keep.tile([P, H], BF16)
+        bias_rows = keep.tile([P, 8 * H], BF16)
+        ones = keep.tile([P, P], BF16)
+        identity = keep.tile([P, P], F32)
+        x_codes = keep.tile([P, GROUPS + 1, P], U32, align_bytes=64)
+        x_scales = keep.tile([P, GROUPS + 1, P], U8, align_bytes=64)
+        words = [
+            [keep.tile([P, GROUPS, H], U32, align_bytes=64, name="words_%d_%d" % (gate, branch)) for branch in (LIGHT, TEMP)]
+            for gate in range(4)
+        ]
+        planes = keep.tile([P, 2, GROUPS, H], U8, align_bytes=64)
+
+        nc.vector.memset(planes[:].rearrange("p b g n -> p (b g n)").bitcast(I32), 0)
+        nc.vector.memset(bias_rows[:].bitcast(I32), 0)
+        nc.vector.memset(ones[:], 1.0)
+        make_identity(nc, identity[:])
+
+        nc.scalar.dma_start(out=hx_light[:, 0:H], in_=h_light)
+        nc.scalar.dma_start(out=hx_temp0[:, 0:H], in_=h_temp)
+        nc.scalar.dma_start(out=hx_temp0[:, H:K_PASS], in_=y[:, 0 : K_PASS - H])
+        for gate in range(4):
+            for branch in (LIGHT, TEMP):
+                col = (2 * gate + branch) * H
+                nc.scalar.dma_start(out=bias_rows[0:1, col : col + H], in_=w_bias[gate][branch].unsqueeze(0))
+        nc.scalar.dma_start(out=c_bf16[:], in_=c_light)
+
+        y_cols = GROUPS_PER_Y_LOAD * K_PASS
+        for first in range(0, K, y_cols):
+            lo = max(first, H)
+            nc.sync.dma_start(out=hx_light[:, lo : first + y_cols], in_=y[:, lo - H : first + y_cols - H])
+
+        for gate in range(4):
+            for branch in (LIGHT, TEMP):
+                rows = w_scales[gate][branch].bitcast(I32).rearrange("g (q r) n -> r q g n", r=4)
+                for r in range(4):
+                    nc.sync.dma_start(out=planes[4 * gate + r : P : 32, branch, :, :].bitcast(I32), in_=rows[r])
+
+        for gate in range(4):
+            for branch in (LIGHT, TEMP):
+                by_partition = w_words[gate][branch].rearrange("g p n t -> p g (n t)").bitcast(I32)
+                for g in range(0, GROUPS, GROUPS_PER_W_LOAD):
+                    some = slice(g, g + GROUPS_PER_W_LOAD)
+                    nc.sync.dma_start(out=words[gate][branch][:, some, :].bitcast(I32), in_=by_partition[:, some, :])
+
+        def transpose_and_quantise(x_bf16, slot, groups):
+            x_words = x_bf16.bitcast(F32)
+            flipped = t_psum.tile([P, groups, 2, P], F32)
+            for j in range(groups):
+                for u in range(2):
+                    nc.tensor.transpose(
+                        out=flipped[:, j, u, :],
+                        in_=x_words[:, WORDS * j + u : WORDS * (j + 1) : 2],
+                        identity=identity[:],
+                    )
+            grouped = stage.tile([P, groups * P * 4], BF16, align_bytes=64)
+            nc.scalar.copy(
+                out=grouped[:].bitcast(F32).rearrange("p (j r u) -> p j r u", j=groups, u=2),
+                in_=flipped[:].rearrange("p j u r -> p j r u"),
+            )
+            nc.vector.quantize_mx(
+                out=x_codes[:, slot : slot + groups, :].rearrange("p j r -> p (j r)").bitcast(FP8X4),
+                scales=x_scales[:, slot : slot + groups, :].rearrange("p j r -> p (j r)"),
+                in_=grouped[:],
+            )
+
+        for g in range(0, GROUPS, GROUPS_PER_ROUND):
+            transpose_and_quantise(hx_light[:, K_PASS * g : K_PASS * (g + GROUPS_PER_ROUND)], g, GROUPS_PER_ROUND)
+        transpose_and_quantise(hx_temp0[:], TEMP_SLOT, 1)
+
+        bias_all = keep.tile([P, 4, 2, H], F32)
+        for gate in range(4):
+            spread = b_psum.tile([P, 2 * H], F32)
+            nc.tensor.matmul(
+                out=spread[:], lhsT=ones[:], rhs=bias_rows[:, 2 * H * gate : 2 * H * (gate + 1)], start=True, stop=True
+            )
+            nc.vector.tensor_copy(out=bias_all[:, gate, :, :].rearrange("p b n -> p (b n)"), in_=spread[:])
+        c_f32 = keep.tile([P, H], F32)
+        nc.vector.tensor_copy(out=c_f32[:], in_=c_bf16[:])
+
+        def gate_values(gate, func):
+            values = keep.tile([P, 2, H], F32, name="values_%d" % gate)
+            for branch in (LIGHT, TEMP):
+                z_sum = z_psum.tile([P, H], F32)
+                for g in range(GROUPS):
+                    slot = TEMP_SLOT if (branch == TEMP and g == 0) else g
+                    nc.tensor.matmul_mx(
+                        out=z_sum[:],
+                        lhsT=x_codes[:, slot, :].bitcast(FP8X4),
+                        lhsT_scale=x_scales[:, slot, :],
+                        rhs=words[gate][branch][:, g, :].bitcast(FP8X4),
+                        rhs_scale=planes[4 * gate : P, branch, g, :],
+                        start=(g == 0),
+                        stop=(g == GROUPS - 1),
+                    )
+                z = stage.tile([P, H], F32)
+                nc.vector.tensor_add(out=z[:], in0=z_sum[:], in1=bias_all[:, gate, branch, :])
+                nc.scalar.activation(out=values[:, branch, :], in_=z[:], func=func)
+            return values
+
+        f = gate_values(GATE_F, ACT.Sigmoid)
+        f_sum = keep.tile([P, H], F32)
+        nc.vector.tensor_add(out=f_sum[:], in0=f[:, LIGHT, :], in1=f[:, TEMP, :])
+        kept = keep.tile([P, H], F32)
+        nc.vector.tensor_mul(out=kept[:], in0=f_sum[:], in1=c_f32[:])
+
+        i = gate_values(GATE_I, ACT.Sigmoid)
+        ch = gate_values(GATE_C, ACT.Tanh)
+        fresh = keep.tile([P, 2, H], F32)
+        nc.vector.tensor_mul(out=fresh[:], in0=i[:], in1=ch[:])
+        fresh_sum = keep.tile([P, H], F32)
+        nc.vector.tensor_add(out=fresh_sum[:], in0=fresh[:, LIGHT, :], in1=fresh[:, TEMP, :])
+        c_new = keep.tile([P, H], F32)
+        nc.vector.tensor_add(out=c_new[:], in0=kept[:], in1=fresh_sum[:])
+        tanh_c = keep.tile([P, H], F32)
+        nc.scalar.activation(out=tanh_c[:], in_=c_new[:], func=ACT.Tanh)
+        nc.scalar.dma_start(out=out_c, in_=c_new[:])
+
+        o = gate_values(GATE_O, ACT.Sigmoid)
+        o_sum = keep.tile([P, H], F32)
+        nc.vector.tensor_add(out=o_sum[:], in0=o[:, LIGHT, :], in1=o[:, TEMP, :])
+        h_new = keep.tile([P, H], F32)
+        nc.vector.tensor_mul(out=h_new[:], in0=o_sum[:], in1=tanh_c[:])
+        nc.sync.dma_start(out=out_h, in_=h_new[:])

@@ -63,6 +63,12 @@ def tile_customlstmcell_k_kernel(tc, y, h_light, c_light, h_temp, c_temp, *weigh
         nc.vector.memset(ones[:], 1.0)
         make_identity(nc, identity[:])
 
+        for gate in range(4):
+            for branch in (LIGHT, TEMP):
+                rows = w_scales[gate][branch].bitcast(F32).rearrange("g (q r) n -> r q g n", r=4)
+                for r in range(4):
+                    nc.gpsimd.dma_start(out=planes[4 * gate + r : P : 32, branch, :, :].bitcast(F32), in_=rows[r])
+
         nc.scalar.dma_start(out=hx_light[:, 0:H], in_=h_light)
         nc.scalar.dma_start(out=hx_temp0[:, 0:H], in_=h_temp)
         nc.scalar.dma_start(out=hx_temp0[:, H:K_PASS], in_=y[:, 0 : K_PASS - H])
@@ -76,12 +82,6 @@ def tile_customlstmcell_k_kernel(tc, y, h_light, c_light, h_temp, c_temp, *weigh
         for first in range(0, K, y_cols):
             lo = max(first, H)
             nc.sync.dma_start(out=hx_light[:, lo : first + y_cols], in_=y[:, lo - H : first + y_cols - H])
-
-        for gate in range(4):
-            for branch in (LIGHT, TEMP):
-                rows = w_scales[gate][branch].bitcast(I32).rearrange("g (q r) n -> r q g n", r=4)
-                for r in range(4):
-                    nc.sync.dma_start(out=planes[4 * gate + r : P : 32, branch, :, :].bitcast(I32), in_=rows[r])
 
         for gate in range(4):
             for branch in (LIGHT, TEMP):

@@ -56,18 +56,23 @@ def tile_customlstmcell_k_kernel(tc, y, h_light, c_light, h_temp, c_temp, *weigh
             [keep.tile([P, GROUPS, H], U32, align_bytes=64, name="words_%d_%d" % (gate, branch)) for branch in (LIGHT, TEMP)]
             for gate in range(4)
         ]
-        planes = keep.tile([P, 2, GROUPS, H], U8, align_bytes=64)
+        planes = [
+            [keep.tile([P, GROUPS, H], U8, align_bytes=64, name="planes_%d_%d" % (gate, branch)) for branch in (LIGHT, TEMP)]
+            for gate in range(4)
+        ]
 
-        nc.vector.memset(planes[:].rearrange("p b g n -> p (b g n)").bitcast(I32), 0)
+        make_identity(nc, identity[:])
         nc.vector.memset(bias_rows[:].bitcast(I32), 0)
         nc.vector.memset(ones[:], 1.0)
-        make_identity(nc, identity[:])
+        for gate in range(4):
+            for branch in (LIGHT, TEMP):
+                nc.vector.memset(planes[gate][branch][:].rearrange("p g n -> p (g n)").bitcast(I32), 0)
 
         for gate in range(4):
             for branch in (LIGHT, TEMP):
                 rows = w_scales[gate][branch].bitcast(F32).rearrange("g (q r) n -> r q g n", r=4)
                 for r in range(4):
-                    nc.gpsimd.dma_start(out=planes[4 * gate + r : P : 32, branch, :, :].bitcast(F32), in_=rows[r])
+                    nc.gpsimd.dma_start(out=planes[gate][branch][4 * gate + r : P : 32, :, :].bitcast(F32), in_=rows[r])
 
         nc.scalar.dma_start(out=hx_light[:, 0:H], in_=h_light)
         nc.scalar.dma_start(out=hx_temp0[:, 0:H], in_=h_temp)
@@ -136,7 +141,7 @@ def tile_customlstmcell_k_kernel(tc, y, h_light, c_light, h_temp, c_temp, *weigh
                         lhsT=x_codes[:, slot, :].bitcast(FP8X4),
                         lhsT_scale=x_scales[:, slot, :],
                         rhs=words[gate][branch][:, g, :].bitcast(FP8X4),
-                        rhs_scale=planes[4 * gate : P, branch, g, :],
+                        rhs_scale=planes[gate][branch][4 * gate : P, g, :],
                         start=(g == 0),
                         stop=(g == GROUPS - 1),
                     )

@@ -68,11 +68,14 @@ def tile_customlstmcell_k_kernel(tc, y, h_light, c_light, h_temp, c_temp, *weigh
             for branch in (LIGHT, TEMP):
                 nc.vector.memset(planes[gate][branch][:].rearrange("p g n -> p (g n)").bitcast(I32), 0)
 
-        for gate in range(4):
+        def load_scales(queue, as_dtype, gate):
             for branch in (LIGHT, TEMP):
-                rows = w_scales[gate][branch].bitcast(F32).rearrange("g (q r) n -> r q g n", r=4)
+                rows = w_scales[gate][branch].bitcast(as_dtype).rearrange("g (q r) n -> r q g n", r=4)
                 for r in range(4):
-                    nc.gpsimd.dma_start(out=planes[gate][branch][4 * gate + r : P : 32, :, :].bitcast(F32), in_=rows[r])
+                    queue.dma_start(out=planes[gate][branch][4 * gate + r : P : 32, :, :].bitcast(as_dtype), in_=rows[r])
+
+        for gate in (GATE_I, GATE_C, GATE_O):
+            load_scales(nc.gpsimd, F32, gate)
 
         nc.scalar.dma_start(out=hx_light[:, 0:H], in_=h_light)
         nc.scalar.dma_start(out=hx_temp0[:, 0:H], in_=h_temp)
@@ -88,6 +91,7 @@ def tile_customlstmcell_k_kernel(tc, y, h_light, c_light, h_temp, c_temp, *weigh
             lo = max(first, H)
             nc.sync.dma_start(out=hx_light[:, lo : first + y_cols], in_=y[:, lo - H : first + y_cols - H])
 
+        load_scales(nc.sync, I32, GATE_F)
         for gate in range(4):
             for branch in (LIGHT, TEMP):
                 by_partition = w_words[gate][branch].rearrange("g p n t -> p g (n t)").bitcast(I32)

@@ -62,42 +62,62 @@ def tile_customlstmcell_k_kernel(tc, y, h_light, c_light, h_temp, c_temp, *weigh
         ]
 
         make_identity(nc, identity[:])
-        nc.vector.memset(bias_rows[:].bitcast(I32), 0)
-        nc.vector.memset(ones[:], 1.0)
-        for gate in range(4):
+
+        def zero_planes(gate):
             for branch in (LIGHT, TEMP):
                 nc.vector.memset(planes[gate][branch][:].rearrange("p g n -> p (g n)").bitcast(I32), 0)
 
-        def load_scales(queue, as_dtype, gate):
-            for branch in (LIGHT, TEMP):
-                rows = w_scales[gate][branch].bitcast(as_dtype).rearrange("g (q r) n -> r q g n", r=4)
-                for r in range(4):
-                    queue.dma_start(out=planes[gate][branch][4 * gate + r : P : 32, :, :].bitcast(as_dtype), in_=rows[r])
+        zero_planes(GATE_F)
+        zero_planes(GATE_I)
+        nc.vector.memset(bias_rows[:].bitcast(I32), 0)
+        nc.vector.memset(ones[:], 1.0)
+        zero_planes(GATE_C)
+        zero_planes(GATE_O)
+
+        def load_scales(queue, gate, branch, r):
+            rows = w_scales[gate][branch].bitcast(F32).rearrange("g (q r) n -> r q g n", r=4)
+            queue.dma_start(out=planes[gate][branch][4 * gate + r : P : 32, :, :].bitcast(F32), in_=rows[r])
+
+        def load_bias(gate, branch):
+            col = (2 * gate + branch) * H
+            nc.scalar.dma_start(out=bias_rows[0:1, col : col + H], in_=w_bias[gate][branch].unsqueeze(0))
+
+        def load_y(chunk):
+            first = chunk * GROUPS_PER_Y_LOAD * K_PASS
+            lo = max(first, H)
+            hi = first + GROUPS_PER_Y_LOAD * K_PASS
+            nc.sync.dma_start(out=hx_light[:, lo:hi], in_=y[:, lo - H : hi - H])
+
+        def load_words(number):
+            gate, branch, part = number // 8, (number // 4) % 2, number % 4
+            by_partition = w_words[gate][branch].rearrange("g p n t -> p g (n t)").bitcast(I32)
+            some = slice(part * GROUPS_PER_W_LOAD, (part + 1) * GROUPS_PER_W_LOAD)
+            nc.sync.dma_start(out=words[gate][branch][:, some, :].bitcast(I32), in_=by_partition[:, some, :])
 
         for gate in (GATE_I, GATE_C, GATE_O):
-            load_scales(nc.gpsimd, F32, gate)
-
-        nc.scalar.dma_start(out=hx_light[:, 0:H], in_=h_light)
-        nc.scalar.dma_start(out=hx_temp0[:, 0:H], in_=h_temp)
-        nc.scalar.dma_start(out=hx_temp0[:, H:K_PASS], in_=y[:, 0 : K_PASS - H])
-        for gate in range(4):
             for branch in (LIGHT, TEMP):
-                col = (2 * gate + branch) * H
-                nc.scalar.dma_start(out=bias_rows[0:1, col : col + H], in_=w_bias[gate][branch].unsqueeze(0))
-        nc.scalar.dma_start(out=c_bf16[:], in_=c_light)
+                for r in range(4):
+                    load_scales(nc.gpsimd, gate, branch, r)
 
-        y_cols = GROUPS_PER_Y_LOAD * K_PASS
-        for first in range(0, K, y_cols):
-            lo = max(first, H)
-            nc.sync.dma_start(out=hx_light[:, lo : first + y_cols], in_=y[:, lo - H : first + y_cols - H])
+        def dma_round(small_before, large, small_after):
+            for start in small_before:
+                start()
+            for start in large:
+                start()
+            for start in small_after:
+                start()
 
-        load_scales(nc.sync, I32, GATE_F)
-        for gate in range(4):
-            for branch in (LIGHT, TEMP):
-                by_partition = w_words[gate][branch].rearrange("g p n t -> p g (n t)").bitcast(I32)
-                for g in range(0, GROUPS, GROUPS_PER_W_LOAD):
-                    some = slice(g, g + GROUPS_PER_W_LOAD)
-                    nc.sync.dma_start(out=words[gate][branch][:, some, :].bitcast(I32), in_=by_partition[:, some, :])
+        dma_round(
+            [lambda: nc.scalar.dma_start(out=hx_light[:, 0:H], in_=h_light),
+             lambda: nc.scalar.dma_start(out=hx_temp0[:, 0:H], in_=h_temp)],
+            [lambda c=c: load_y(c) for c in range(4)],
+            [lambda r=r: load_scales(nc.scalar, GATE_F, LIGHT, r) for r in (0, 1)],
+        )
+        dma_round(
+            [lambda r=r: load_scales(nc.scalar, GATE_F, LIGHT, r) for r in (2, 3)],
+            [lambda n=n: load_words(n) for n in range(0, 4)],
+            [lambda r=r: load_scales(nc.scalar, GATE_F, TEMP, r) for r in (0, 1)],
+        )
 
         def transpose_and_quantise(x_bf16, slot, groups):
             x_words = x_bf16.bitcast(F32)
@@ -120,19 +140,42 @@ def tile_customlstmcell_k_kernel(tc, y, h_light, c_light, h_temp, c_temp, *weigh
                 in_=grouped[:],
             )
 
-        for g in range(0, GROUPS, GROUPS_PER_ROUND):
-            transpose_and_quantise(hx_light[:, K_PASS * g : K_PASS * (g + GROUPS_PER_ROUND)], g, GROUPS_PER_ROUND)
+        def prepare_light(rounds):
+            for g in rounds:
+                transpose_and_quantise(hx_light[:, K_PASS * g : K_PASS * (g + GROUPS_PER_ROUND)], g, GROUPS_PER_ROUND)
+
+        prepare_light((0, 2, 4))
+        dma_round(
+            [lambda r=r: load_scales(nc.scalar, GATE_F, TEMP, r) for r in (2, 3)],
+            [lambda n=n: load_words(n) for n in range(4, 8)],
+            [lambda b=b: load_bias(GATE_F, b) for b in (LIGHT, TEMP)],
+        )
+        prepare_light((6, 8, 10, 12, 14))
+        dma_round(
+            [lambda b=b: load_bias(GATE_I, b) for b in (LIGHT, TEMP)],
+            [lambda n=n: load_words(n) for n in range(8, 12)],
+            [lambda b=b: load_bias(GATE_C, b) for b in (LIGHT, TEMP)],
+        )
+        nc.vector.tensor_copy(out=hx_temp0[:, H:K_PASS], in_=hx_light[:, H:K_PASS])
         transpose_and_quantise(hx_temp0[:], TEMP_SLOT, 1)
+        dma_round(
+            [lambda b=b: load_bias(GATE_O, b) for b in (LIGHT, TEMP)],
+            [lambda n=n: load_words(n) for n in range(12, 16)],
+            [lambda: nc.scalar.dma_start(out=c_bf16[:], in_=c_light)],
+        )
+        for n in range(16, 32):
+            load_words(n)
 
         bias_all = keep.tile([P, 4, 2, H], F32)
-        for gate in range(4):
+
+        def spread_bias(gate):
             spread = b_psum.tile([P, 2 * H], F32)
             nc.tensor.matmul(
                 out=spread[:], lhsT=ones[:], rhs=bias_rows[:, 2 * H * gate : 2 * H * (gate + 1)], start=True, stop=True
             )
             nc.vector.tensor_copy(out=bias_all[:, gate, :, :].rearrange("p b n -> p (b n)"), in_=spread[:])
+
         c_f32 = keep.tile([P, H], F32)
-        nc.vector.tensor_copy(out=c_f32[:], in_=c_bf16[:])
 
         def gate_values(gate, func):
             values = keep.tile([P, 2, H], F32, name="values_%d" % gate)
@@ -149,12 +192,15 @@ def tile_customlstmcell_k_kernel(tc, y, h_light, c_light, h_temp, c_temp, *weigh
                         start=(g == 0),
                         stop=(g == GROUPS - 1),
                     )
+                    if branch == LIGHT and g == GROUPS - GROUPS_PER_W_LOAD - 1:
+                        spread_bias(gate)
                 z = stage.tile([P, H], F32)
                 nc.vector.tensor_add(out=z[:], in0=z_sum[:], in1=bias_all[:, gate, branch, :])
                 nc.scalar.activation(out=values[:, branch, :], in_=z[:], func=func)
             return values
 
         f = gate_values(GATE_F, ACT.Sigmoid)
+        nc.vector.tensor_copy(out=c_f32[:], in_=c_bf16[:])
         f_sum = keep.tile([P, H], F32)
         nc.vector.tensor_add(out=f_sum[:], in0=f[:, LIGHT, :], in1=f[:, TEMP, :])
         kept = keep.tile([P, H], F32)

@@ -24,6 +24,7 @@ GATE_F, GATE_I, GATE_C, GATE_O = 0, 1, 2, 3
 GROUPS_PER_ROUND = 2
 GROUPS_PER_Y_LOAD = 4
 GROUPS_PER_W_LOAD = 4
+LAST_PIECES = 2
 TEMP_SLOT = GROUPS
 
 FLOPS = 2 * P * K * 8 * H
@@ -88,11 +89,14 @@ def tile_customlstmcell_k_kernel(tc, y, h_light, c_light, h_temp, c_temp, *weigh
             hi = first + GROUPS_PER_Y_LOAD * K_PASS
             nc.sync.dma_start(out=hx_light[:, lo:hi], in_=y[:, lo - H : hi - H])
 
+        def load_groups(gate, branch, first, count):
+            by_partition = w_words[gate][branch].rearrange("g p n t -> p g (n t)").bitcast(I32)
+            some = slice(first, first + count)
+            nc.sync.dma_start(out=words[gate][branch][:, some, :].bitcast(I32), in_=by_partition[:, some, :])
+
         def load_words(number):
             gate, branch, part = number // 8, (number // 4) % 2, number % 4
-            by_partition = w_words[gate][branch].rearrange("g p n t -> p g (n t)").bitcast(I32)
-            some = slice(part * GROUPS_PER_W_LOAD, (part + 1) * GROUPS_PER_W_LOAD)
-            nc.sync.dma_start(out=words[gate][branch][:, some, :].bitcast(I32), in_=by_partition[:, some, :])
+            load_groups(gate, branch, part * GROUPS_PER_W_LOAD, GROUPS_PER_W_LOAD)
 
         for gate in (GATE_I, GATE_C, GATE_O):
             for branch in (LIGHT, TEMP):
@@ -163,8 +167,11 @@ def tile_customlstmcell_k_kernel(tc, y, h_light, c_light, h_temp, c_temp, *weigh
             [lambda n=n: load_words(n) for n in range(12, 16)],
             [lambda: nc.scalar.dma_start(out=c_bf16[:], in_=c_light)],
         )
-        for n in range(16, 32):
+        for n in range(16, 31):
             load_words(n)
+        load_groups(GATE_O, TEMP, 12, 2)
+        load_groups(GATE_O, TEMP, 14, 1)
+        load_groups(GATE_O, TEMP, 15, 1)
 
         bias_all = keep.tile([P, 4, 2, H], F32)
 
@@ -176,6 +183,9 @@ def tile_customlstmcell_k_kernel(tc, y, h_light, c_light, h_temp, c_temp, *weigh
             nc.vector.tensor_copy(out=bias_all[:, gate, :, :].rearrange("p b n -> p (b n)"), in_=spread[:])
 
         c_f32 = keep.tile([P, H], F32)
+
+        def column_pieces(pieces):
+            return [slice(H * piece // pieces, H * (piece + 1) // pieces) for piece in range(pieces)]
 
         def gate_values(gate, func):
             values = keep.tile([P, 2, H], F32, name="values_%d" % gate)
@@ -195,8 +205,11 @@ def tile_customlstmcell_k_kernel(tc, y, h_light, c_light, h_temp, c_temp, *weigh
                     if branch == LIGHT and g == GROUPS - GROUPS_PER_W_LOAD - 1:
                         spread_bias(gate)
                 z = stage.tile([P, H], F32)
-                nc.vector.tensor_add(out=z[:], in0=z_sum[:], in1=bias_all[:, gate, branch, :])
-                nc.scalar.activation(out=values[:, branch, :], in_=z[:], func=func)
+                pieces = LAST_PIECES if (gate == GATE_O and branch == TEMP) else 1
+                for cols in column_pieces(pieces):
+                    nc.vector.tensor_add(out=z[:, cols], in0=z_sum[:, cols], in1=bias_all[:, gate, branch, cols])
+                for cols in column_pieces(pieces):
+                    nc.scalar.activation(out=values[:, branch, cols], in_=z[:, cols], func=func)
             return values
 
         f = gate_values(GATE_F, ACT.Sigmoid)
@@ -220,7 +233,9 @@ def tile_customlstmcell_k_kernel(tc, y, h_light, c_light, h_temp, c_temp, *weigh
 
         o = gate_values(GATE_O, ACT.Sigmoid)
         o_sum = keep.tile([P, H], F32)
-        nc.vector.tensor_add(out=o_sum[:], in0=o[:, LIGHT, :], in1=o[:, TEMP, :])
         h_new = keep.tile([P, H], F32)
-        nc.vector.tensor_mul(out=h_new[:], in0=o_sum[:], in1=tanh_c[:])
+        for cols in column_pieces(LAST_PIECES):
+            nc.vector.tensor_add(out=o_sum[:, cols], in0=o[:, LIGHT, cols], in1=o[:, TEMP, cols])
+        for cols in column_pieces(LAST_PIECES):
+            nc.vector.tensor_mul(out=h_new[:, cols], in0=o_sum[:, cols], in1=tanh_c[:, cols])
         nc.sync.dma_start(out=out_h, in_=h_new[:])

@@ -24,6 +24,7 @@ GATE_F, GATE_I, GATE_C, GATE_O = 0, 1, 2, 3
 GROUPS_PER_ROUND = 2
 GROUPS_PER_Y_LOAD = 4
 GROUPS_PER_W_LOAD = 4
+DMA_ALIGN = 256
 LAST_PIECES = 2
 TEMP_SLOT = GROUPS
 
@@ -45,8 +46,8 @@ def tile_customlstmcell_k_kernel(tc, y, h_light, c_light, h_temp, c_temp, *weigh
         z_psum = ctx.enter_context(tc.psum_pool(name="z_psum", bufs=3))
         ctx.enter_context(tc.manual_schedule())
 
-        hx_light = keep.tile([P, K], BF16)
-        hx_temp0 = keep.tile([P, K_PASS], BF16)
+        hx_light = keep.tile([P, K], BF16, align_bytes=DMA_ALIGN)
+        hx_temp0 = keep.tile([P, K_PASS], BF16, align_bytes=DMA_ALIGN)
         c_bf16 = keep.tile([P, H], BF16)
         bias_rows = keep.tile([P, 8 * H], BF16)
         ones = keep.tile([P, P], BF16)
@@ -54,11 +55,11 @@ def tile_customlstmcell_k_kernel(tc, y, h_light, c_light, h_temp, c_temp, *weigh
         x_codes = keep.tile([P, GROUPS + 1, P], U32, align_bytes=64)
         x_scales = keep.tile([P, GROUPS + 1, P], U8, align_bytes=64)
         words = [
-            [keep.tile([P, GROUPS, H], U32, align_bytes=64, name="words_%d_%d" % (gate, branch)) for branch in (LIGHT, TEMP)]
+            [keep.tile([P, GROUPS, H], U32, align_bytes=DMA_ALIGN, name="words_%d_%d" % (gate, branch)) for branch in (LIGHT, TEMP)]
             for gate in range(4)
         ]
         planes = [
-            [keep.tile([P, GROUPS, H], U8, align_bytes=64, name="planes_%d_%d" % (gate, branch)) for branch in (LIGHT, TEMP)]
+            [keep.tile([P, GROUPS, H], U8, align_bytes=DMA_ALIGN, name="planes_%d_%d" % (gate, branch)) for branch in (LIGHT, TEMP)]
             for gate in range(4)
         ]
 
@@ -225,7 +226,7 @@ def tile_customlstmcell_k_kernel(tc, y, h_light, c_light, h_temp, c_temp, *weigh
         nc.vector.tensor_mul(out=fresh[:], in0=i[:], in1=ch[:])
         fresh_sum = keep.tile([P, H], F32)
         nc.vector.tensor_add(out=fresh_sum[:], in0=fresh[:, LIGHT, :], in1=fresh[:, TEMP, :])
-        c_new = keep.tile([P, H], F32)
+        c_new = keep.tile([P, H], F32, align_bytes=DMA_ALIGN)
         nc.vector.tensor_add(out=c_new[:], in0=kept[:], in1=fresh_sum[:])
         tanh_c = keep.tile([P, H], F32)
         nc.scalar.activation(out=tanh_c[:], in_=c_new[:], func=ACT.Tanh)
@@ -233,7 +234,7 @@ def tile_customlstmcell_k_kernel(tc, y, h_light, c_light, h_temp, c_temp, *weigh
 
         o = gate_values(GATE_O, ACT.Sigmoid)
         o_sum = keep.tile([P, H], F32)
-        h_new = keep.tile([P, H], F32)
+        h_new = keep.tile([P, H], F32, align_bytes=DMA_ALIGN)
         for cols in column_pieces(LAST_PIECES):
             nc.vector.tensor_add(out=o_sum[:, cols], in0=o[:, LIGHT, cols], in1=o[:, TEMP, cols])
         for cols in column_pieces(LAST_PIECES):

@@ -25,6 +25,7 @@ GROUPS_PER_ROUND = 2
 GROUPS_PER_Y_LOAD = 4
 GROUPS_PER_W_LOAD = 4
 DMA_ALIGN = 256
+WORDS_ALIGN = 1024
 LAST_PIECES = 2
 TEMP_SLOT = GROUPS
 
@@ -55,7 +56,7 @@ def tile_customlstmcell_k_kernel(tc, y, h_light, c_light, h_temp, c_temp, *weigh
         x_codes = keep.tile([P, GROUPS + 1, P], U32, align_bytes=64)
         x_scales = keep.tile([P, GROUPS + 1, P], U8, align_bytes=64)
         words = [
-            [keep.tile([P, GROUPS, H], U32, align_bytes=DMA_ALIGN, name="words_%d_%d" % (gate, branch)) for branch in (LIGHT, TEMP)]
+            [keep.tile([P, GROUPS, H], U32, align_bytes=WORDS_ALIGN, name="words_%d_%d" % (gate, branch)) for branch in (LIGHT, TEMP)]
             for gate in range(4)
         ]
         planes = [

@@ -23,7 +23,10 @@ GATE_F, GATE_I, GATE_C, GATE_O = 0, 1, 2, 3
 
 GROUPS_PER_ROUND = 2
 GROUPS_PER_Y_LOAD = 4
-GROUPS_PER_W_LOAD = 4
+GROUPS_PER_W_LOAD = 8
+LAST_WEIGHT_LOADS = ((0, 4), (4, 4), (8, 4), (12, 2), (14, 1), (15, 1))
+SMALL_PER_GAP = 2
+SPREAD_BIAS_BEHIND = 11
 DMA_ALIGN = 256
 WORDS_ALIGN = 1024
 LAST_PIECES = 2
@@ -77,13 +80,13 @@ def tile_customlstmcell_k_kernel(tc, y, h_light, c_light, h_temp, c_temp, *weigh
         zero_planes(GATE_C)
         zero_planes(GATE_O)
 
-        def load_scales(queue, gate, branch, r):
-            rows = w_scales[gate][branch].bitcast(F32).rearrange("g (q r) n -> r q g n", r=4)
-            queue.dma_start(out=planes[gate][branch][4 * gate + r : P : 32, :, :].bitcast(F32), in_=rows[r])
+        def load_scales(queue, view, gate, branch, r):
+            rows = w_scales[gate][branch].bitcast(view).rearrange("g (q r) n -> r q g n", r=4)
+            queue.dma_start(out=planes[gate][branch][4 * gate + r : P : 32, :, :].bitcast(view), in_=rows[r])
 
         def load_bias(gate, branch):
             col = (2 * gate + branch) * H
-            nc.scalar.dma_start(out=bias_rows[0:1, col : col + H], in_=w_bias[gate][branch].unsqueeze(0))
+            nc.sync.dma_start(out=bias_rows[0:1, col : col + H], in_=w_bias[gate][branch].unsqueeze(0))
 
         def load_y(chunk):
             first = chunk * GROUPS_PER_Y_LOAD * K_PASS
@@ -96,34 +99,30 @@ def tile_customlstmcell_k_kernel(tc, y, h_light, c_light, h_temp, c_temp, *weigh
             some = slice(first, first + count)
             nc.sync.dma_start(out=words[gate][branch][:, some, :].bitcast(I32), in_=by_partition[:, some, :])
 
-        def load_words(number):
-            gate, branch, part = number // 8, (number // 4) % 2, number % 4
-            load_groups(gate, branch, part * GROUPS_PER_W_LOAD, GROUPS_PER_W_LOAD)
-
         for gate in (GATE_I, GATE_C, GATE_O):
             for branch in (LIGHT, TEMP):
                 for r in range(4):
-                    load_scales(nc.gpsimd, gate, branch, r)
+                    load_scales(nc.gpsimd, F32, gate, branch, r)
 
-        def dma_round(small_before, large, small_after):
-            for start in small_before:
+        nc.sync.dma_start(out=hx_light[:, 0:H], in_=h_light)
+        for chunk in range(GROUPS // GROUPS_PER_Y_LOAD):
+            load_y(chunk)
+        nc.sync.dma_start(out=hx_temp0[:, 0:H], in_=h_temp)
+        small = [lambda b=b, r=r: load_scales(nc.sync, I32, GATE_F, b, r) for b in (LIGHT, TEMP) for r in range(4)]
+        small += [lambda g=g, b=b: load_bias(g, b) for g in range(4) for b in (LIGHT, TEMP)]
+        small += [lambda: nc.sync.dma_start(out=c_bf16[:], in_=c_light)]
+        word_loads = [
+            (gate, branch, first, GROUPS_PER_W_LOAD)
+            for gate in range(4)
+            for branch in (LIGHT, TEMP)
+            for first in range(0, GROUPS, GROUPS_PER_W_LOAD)
+            if (gate, branch) != (GATE_O, TEMP)
+        ]
+        word_loads += [(GATE_O, TEMP, first, count) for first, count in LAST_WEIGHT_LOADS]
+        for number, load in enumerate(word_loads):
+            load_groups(*load)
+            for start in small[number * SMALL_PER_GAP : (number + 1) * SMALL_PER_GAP]:
                 start()
-            for start in large:
-                start()
-            for start in small_after:
-                start()
-
-        dma_round(
-            [lambda: nc.scalar.dma_start(out=hx_light[:, 0:H], in_=h_light),
-             lambda: nc.scalar.dma_start(out=hx_temp0[:, 0:H], in_=h_temp)],
-            [lambda c=c: load_y(c) for c in range(4)],
-            [lambda r=r: load_scales(nc.scalar, GATE_F, LIGHT, r) for r in (0, 1)],
-        )
-        dma_round(
-            [lambda r=r: load_scales(nc.scalar, GATE_F, LIGHT, r) for r in (2, 3)],
-            [lambda n=n: load_words(n) for n in range(0, 4)],
-            [lambda r=r: load_scales(nc.scalar, GATE_F, TEMP, r) for r in (0, 1)],
-        )
 
         def transpose_and_quantise(x_bf16, slot, groups):
             x_words = x_bf16.bitcast(F32)
@@ -150,30 +149,9 @@ def tile_customlstmcell_k_kernel(tc, y, h_light, c_light, h_temp, c_temp, *weigh
             for g in rounds:
                 transpose_and_quantise(hx_light[:, K_PASS * g : K_PASS * (g + GROUPS_PER_ROUND)], g, GROUPS_PER_ROUND)
 
-        prepare_light((0, 2, 4))
-        dma_round(
-            [lambda r=r: load_scales(nc.scalar, GATE_F, TEMP, r) for r in (2, 3)],
-            [lambda n=n: load_words(n) for n in range(4, 8)],
-            [lambda b=b: load_bias(GATE_F, b) for b in (LIGHT, TEMP)],
-        )
-        prepare_light((6, 8, 10, 12, 14))
-        dma_round(
-            [lambda b=b: load_bias(GATE_I, b) for b in (LIGHT, TEMP)],
-            [lambda n=n: load_words(n) for n in range(8, 12)],
-            [lambda b=b: load_bias(GATE_C, b) for b in (LIGHT, TEMP)],
-        )
+        prepare_light(range(0, GROUPS, GROUPS_PER_ROUND))
         nc.vector.tensor_copy(out=hx_temp0[:, H:K_PASS], in_=hx_light[:, H:K_PASS])
         transpose_and_quantise(hx_temp0[:], TEMP_SLOT, 1)
-        dma_round(
-            [lambda b=b: load_bias(GATE_O, b) for b in (LIGHT, TEMP)],
-            [lambda n=n: load_words(n) for n in range(12, 16)],
-            [lambda: nc.scalar.dma_start(out=c_bf16[:], in_=c_light)],
-        )
-        for n in range(16, 31):
-            load_words(n)
-        load_groups(GATE_O, TEMP, 12, 2)
-        load_groups(GATE_O, TEMP, 14, 1)
-        load_groups(GATE_O, TEMP, 15, 1)
 
         bias_all = keep.tile([P, 4, 2, H], F32)
 
@@ -204,7 +182,7 @@ def tile_customlstmcell_k_kernel(tc, y, h_light, c_light, h_temp, c_temp, *weigh
                         start=(g == 0),
                         stop=(g == GROUPS - 1),
                     )
-                    if branch == LIGHT and g == GROUPS - GROUPS_PER_W_LOAD - 1:
+                    if branch == LIGHT and g == SPREAD_BIAS_BEHIND:
                         spread_bias(gate)
                 z = stage.tile([P, H], F32)
                 pieces = LAST_PIECES if (gate == GATE_O and branch == TEMP) else 1
@@ -231,7 +209,7 @@ def tile_customlstmcell_k_kernel(tc, y, h_light, c_light, h_temp, c_temp, *weigh
         nc.vector.tensor_add(out=c_new[:], in0=kept[:], in1=fresh_sum[:])
         tanh_c = keep.tile([P, H], F32)
         nc.scalar.activation(out=tanh_c[:], in_=c_new[:], func=ACT.Tanh)
-        nc.scalar.dma_start(out=out_c, in_=c_new[:])
+        nc.sync.dma_start(out=out_c, in_=c_new[:])
 
         o = gate_values(GATE_O, ACT.Sigmoid)
         o_sum = keep.tile([P, H], F32)

from contextlib import ExitStack

import concourse.mybir as mybir
from concourse.masks import make_identity

F32 = mybir.dt.float32
BF16 = mybir.dt.bfloat16
I32 = mybir.dt.int32
U32 = mybir.dt.uint32
U8 = mybir.dt.uint8
FP8X4 = mybir.dt.float8_e4m3fn_x4
ACT = mybir.ActivationFunctionType

P = 128
H = 256
K = 8192
K_PASS = 512
GROUPS = K // K_PASS
WORDS = K_PASS // 2

LIGHT, TEMP = 0, 1
GATE_F, GATE_I, GATE_C, GATE_O = 0, 1, 2, 3

GROUPS_PER_ROUND = 2
GROUPS_PER_Y_LOAD = 4
GROUPS_PER_W_LOAD = 8
LAST_WEIGHT_LOADS = ((0, 4), (4, 4), (8, 4), (12, 2), (14, 1), (15, 1))
SMALL_PER_GAP = 2
SPREAD_BIAS_BEHIND = 11
DMA_ALIGN = 256
WORDS_ALIGN = 1024
LAST_PIECES = 2
TEMP_SLOT = GROUPS

FLOPS = 2 * P * K * 8 * H


def tile_customlstmcell_k_kernel(tc, y, h_light, c_light, h_temp, c_temp, *weights_and_outs):
    nc = tc.nc
    w_words = [[weights_and_outs[3 * (4 * branch + gate)] for branch in (LIGHT, TEMP)] for gate in range(4)]
    w_scales = [[weights_and_outs[3 * (4 * branch + gate) + 1] for branch in (LIGHT, TEMP)] for gate in range(4)]
    w_bias = [[weights_and_outs[3 * (4 * branch + gate) + 2] for branch in (LIGHT, TEMP)] for gate in range(4)]
    out_h, out_c = weights_and_outs[24], weights_and_outs[25]

    with ExitStack() as ctx:
        keep = ctx.enter_context(tc.tile_pool(name="keep", bufs=1))
        stage = ctx.enter_context(tc.tile_pool(name="stage", bufs=3))
        t_psum = ctx.enter_context(tc.psum_pool(name="t_psum", bufs=3))
        b_psum = ctx.enter_context(tc.psum_pool(name="b_psum", bufs=2))
        z_psum = ctx.enter_context(tc.psum_pool(name="z_psum", bufs=3))
        ctx.enter_context(tc.manual_schedule())

        hx_light = keep.tile([P, K], BF16, align_bytes=DMA_ALIGN)
        hx_temp0 = keep.tile([P, K_PASS], BF16, align_bytes=DMA_ALIGN)
        c_bf16 = keep.tile([P, H], BF16)
        bias_rows = keep.tile([P, 8 * H], BF16)
        ones = keep.tile([P, P], BF16)
        identity = keep.tile([P, P], F32)
        x_codes = keep.tile([P, GROUPS + 1, P], U32, align_bytes=64)
        x_scales = keep.tile([P, GROUPS + 1, P], U8, align_bytes=64)
        words = [
            [keep.tile([P, GROUPS, H], U32, align_bytes=WORDS_ALIGN, name="words_%d_%d" % (gate, branch)) for branch in (LIGHT, TEMP)]
            for gate in range(4)
        ]
        planes = [
            [keep.tile([P, GROUPS, H], U8, align_bytes=DMA_ALIGN, name="planes_%d_%d" % (gate, branch)) for branch in (LIGHT, TEMP)]
            for gate in range(4)
        ]

        make_identity(nc, identity[:])

        def zero_planes(gate):
            for branch in (LIGHT, TEMP):
                nc.vector.memset(planes[gate][branch][:].rearrange("p g n -> p (g n)").bitcast(I32), 0)

        zero_planes(GATE_F)
        zero_planes(GATE_I)
        nc.vector.memset(bias_rows[:].bitcast(I32), 0)
        nc.vector.memset(ones[:], 1.0)
        zero_planes(GATE_C)
        zero_planes(GATE_O)

        def load_scales(queue, view, gate, branch, r):
            rows = w_scales[gate][branch].bitcast(view).rearrange("g (q r) n -> r q g n", r=4)
            queue.dma_start(out=planes[gate][branch][4 * gate + r : P : 32, :, :].bitcast(view), in_=rows[r])

        def load_bias(gate, branch):
            col = (2 * gate + branch) * H
            nc.sync.dma_start(out=bias_rows[0:1, col : col + H], in_=w_bias[gate][branch].unsqueeze(0))

        def load_y(chunk):
            first = chunk * GROUPS_PER_Y_LOAD * K_PASS
            lo = max(first, H)
            hi = first + GROUPS_PER_Y_LOAD * K_PASS
            nc.sync.dma_start(out=hx_light[:, lo:hi], in_=y[:, lo - H : hi - H])

        def load_groups(gate, branch, first, count):
            by_partition = w_words[gate][branch].rearrange("g p n t -> p g (n t)").bitcast(I32)
            some = slice(first, first + count)
            nc.sync.dma_start(out=words[gate][branch][:, some, :].bitcast(I32), in_=by_partition[:, some, :])

        for gate in (GATE_I, GATE_C, GATE_O):
            for branch in (LIGHT, TEMP):
                for r in range(4):
                    load_scales(nc.gpsimd, F32, gate, branch, r)

        nc.sync.dma_start(out=hx_light[:, 0:H], in_=h_light)
        for chunk in range(GROUPS // GROUPS_PER_Y_LOAD):
            load_y(chunk)
        nc.sync.dma_start(out=hx_temp0[:, 0:H], in_=h_temp)
        small = [lambda b=b, r=r: load_scales(nc.sync, I32, GATE_F, b, r) for b in (LIGHT, TEMP) for r in range(4)]
        small += [lambda g=g, b=b: load_bias(g, b) for g in range(4) for b in (LIGHT, TEMP)]
        small += [lambda: nc.sync.dma_start(out=c_bf16[:], in_=c_light)]
        word_loads = [
            (gate, branch, first, GROUPS_PER_W_LOAD)
            for gate in range(4)
            for branch in (LIGHT, TEMP)
            for first in range(0, GROUPS, GROUPS_PER_W_LOAD)
            if (gate, branch) != (GATE_O, TEMP)
        ]
        word_loads += [(GATE_O, TEMP, first, count) for first, count in LAST_WEIGHT_LOADS]
        for number, load in enumerate(word_loads):
            load_groups(*load)
            for start in small[number * SMALL_PER_GAP : (number + 1) * SMALL_PER_GAP]:
                start()

        def transpose_and_quantise(x_bf16, slot, groups):
            x_words = x_bf16.bitcast(F32)
            flipped = t_psum.tile([P, groups, 2, P], F32)
            for j in range(groups):
                for u in range(2):
                    nc.tensor.transpose(
                        out=flipped[:, j, u, :],
                        in_=x_words[:, WORDS * j + u : WORDS * (j + 1) : 2],
                        identity=identity[:],
                    )
            grouped = stage.tile([P, groups * P * 4], BF16, align_bytes=64)
            nc.scalar.copy(
                out=grouped[:].bitcast(F32).rearrange("p (j r u) -> p j r u", j=groups, u=2),
                in_=flipped[:].rearrange("p j u r -> p j r u"),
            )
            nc.vector.quantize_mx(
                out=x_codes[:, slot : slot + groups, :].rearrange("p j r -> p (j r)").bitcast(FP8X4),
                scales=x_scales[:, slot : slot + groups, :].rearrange("p j r -> p (j r)"),
                in_=grouped[:],
            )

        def prepare_light(rounds):
            for g in rounds:
                transpose_and_quantise(hx_light[:, K_PASS * g : K_PASS * (g + GROUPS_PER_ROUND)], g, GROUPS_PER_ROUND)

        prepare_light(range(0, GROUPS, GROUPS_PER_ROUND))
        nc.vector.tensor_copy(out=hx_temp0[:, H:K_PASS], in_=hx_light[:, H:K_PASS])
        transpose_and_quantise(hx_temp0[:], TEMP_SLOT, 1)

        bias_all = keep.tile([P, 4, 2, H], F32)

        def spread_bias(gate):
            spread = b_psum.tile([P, 2 * H], F32)
            nc.tensor.matmul(
                out=spread[:], lhsT=ones[:], rhs=bias_rows[:, 2 * H * gate : 2 * H * (gate + 1)], start=True, stop=True
            )
            nc.vector.tensor_copy(out=bias_all[:, gate, :, :].rearrange("p b n -> p (b n)"), in_=spread[:])

        c_f32 = keep.tile([P, H], F32)

        def column_pieces(pieces):
            return [slice(H * piece // pieces, H * (piece + 1) // pieces) for piece in range(pieces)]

        def gate_values(gate, func):
            values = keep.tile([P, 2, H], F32, name="values_%d" % gate)
            for branch in (LIGHT, TEMP):
                z_sum = z_psum.tile([P, H], F32)
                for g in range(GROUPS):
                    slot = TEMP_SLOT if (branch == TEMP and g == 0) else g
                    nc.tensor.matmul_mx(
                        out=z_sum[:],
                        lhsT=x_codes[:, slot, :].bitcast(FP8X4),
                        lhsT_scale=x_scales[:, slot, :],
                        rhs=words[gate][branch][:, g, :].bitcast(FP8X4),
                        rhs_scale=planes[gate][branch][4 * gate : P, g, :],
                        start=(g == 0),
                        stop=(g == GROUPS - 1),
                    )
                    if branch == LIGHT and g == SPREAD_BIAS_BEHIND:
                        spread_bias(gate)
                z = stage.tile([P, H], F32)
                pieces = LAST_PIECES if (gate == GATE_O and branch == TEMP) else 1
                for cols in column_pieces(pieces):
                    nc.vector.tensor_add(out=z[:, cols], in0=z_sum[:, cols], in1=bias_all[:, gate, branch, cols])
                for cols in column_pieces(pieces):
                    nc.scalar.activation(out=values[:, branch, cols], in_=z[:, cols], func=func)
            return values

        f = gate_values(GATE_F, ACT.Sigmoid)
        nc.vector.tensor_copy(out=c_f32[:], in_=c_bf16[:])
        f_sum = keep.tile([P, H], F32)
        nc.vector.tensor_add(out=f_sum[:], in0=f[:, LIGHT, :], in1=f[:, TEMP, :])
        kept = keep.tile([P, H], F32)
        nc.vector.tensor_mul(out=kept[:], in0=f_sum[:], in1=c_f32[:])

        i = gate_values(GATE_I, ACT.Sigmoid)
        ch = gate_values(GATE_C, ACT.Tanh)
        fresh = keep.tile([P, 2, H], F32)
        nc.vector.tensor_mul(out=fresh[:], in0=i[:], in1=ch[:])
        fresh_sum = keep.tile([P, H], F32)
        nc.vector.tensor_add(out=fresh_sum[:], in0=fresh[:, LIGHT, :], in1=fresh[:, TEMP, :])
        c_new = keep.tile([P, H], F32, align_bytes=DMA_ALIGN)
        nc.vector.tensor_add(out=c_new[:], in0=kept[:], in1=fresh_sum[:])
        tanh_c = keep.tile([P, H], F32)
        nc.scalar.activation(out=tanh_c[:], in_=c_new[:], func=ACT.Tanh)
        nc.sync.dma_start(out=out_c, in_=c_new[:])

        o = gate_values(GATE_O, ACT.Sigmoid)
        o_sum = keep.tile([P, H], F32)
        h_new = keep.tile([P, H], F32, align_bytes=DMA_ALIGN)
        for cols in column_pieces(LAST_PIECES):
            nc.vector.tensor_add(out=o_sum[:, cols], in0=o[:, LIGHT, cols], in1=o[:, TEMP, cols])
        for cols in column_pieces(LAST_PIECES):
            nc.vector.tensor_mul(out=h_new[:, cols], in0=o_sum[:, cols], in1=tanh_c[:, cols])
        nc.sync.dma_start(out=out_h, in_=h_new[:])
